import numpy as np
import ml_dtypes


def mxq(x, axis, fmt="e4m3"):
    dtype, down = {"e4m3": (ml_dtypes.float8_e4m3fn, 7), "e5m2": (ml_dtypes.float8_e5m2, 14)}[fmt]
    v = np.moveaxis(np.asarray(x, np.float32).astype(ml_dtypes.bfloat16).astype(np.float64), axis, -1)
    blocks = v.reshape(v.shape[:-1] + (-1, 32))
    amax = np.abs(blocks).max(-1, keepdims=True)
    byte = np.maximum(np.where(amax > 0, np.frexp(amax)[1] - 1 + 127, 0) - down, 1)
    scale = np.exp2(byte - 127.0)
    codes = (blocks / scale).astype(np.float32).astype(dtype).astype(np.float64)
    return np.moveaxis((codes * scale).reshape(v.shape), -1, axis)


WIDE = False


def mx_kscale(k):
    if not WIDE:
        return np.ones(k)
    levels = np.array([10, -10, 5, -5, 0])
    a = np.random.permutation(np.resize(levels, k // 512 * 4)).reshape(k // 512, 4)
    idx = np.arange(k)
    return np.exp2(a[idx // 512, idx % 128 // 32])


BF16 = ml_dtypes.bfloat16


def bf(x):
    return np.asarray(x, np.float32).astype(BF16)


def f64(x):
    return np.asarray(x).astype(np.float64)


E2M1 = np.array([0.0, 0.5, 1.0, 1.5, 2.0, 3.0, 4.0, 6.0, -0.0, -0.5, -1.0, -1.5, -2.0, -3.0, -4.0, -6.0])


def pack_weight(w, fmt):
    k, n = w.shape
    w = f64(bf(w)).reshape(k // 32, 32, n)
    amax = np.abs(w).max(1)
    if fmt == "e4m3":
        byte = np.frexp(amax)[1] - 1 + 127 - 7
    else:
        mant, ex = np.frexp(amax / 6.0)
        byte = np.where(mant > 0.5, ex, ex - 1) + 127
    byte = np.clip(np.where(amax > 0, byte, 1), 1, 254)
    scaled = (w * np.exp2(127.0 - byte)[:, None, :]).reshape(k, n).astype(np.float32)
    by_word = np.ascontiguousarray(scaled.reshape(k // 512, 128, 4, n).transpose(0, 1, 3, 2))
    if fmt == "e4m3":
        words = by_word.astype(ml_dtypes.float8_e4m3fn).view(np.uint8)
    else:
        c = by_word.astype(ml_dtypes.float4_e2m1fn).view(np.uint8) & 0xF
        words = c[..., 0::2] | (c[..., 1::2] << 4)
    return np.ascontiguousarray(words), np.ascontiguousarray(byte.astype(np.uint8).reshape(k // 512, 16, n))


def unpack_weight(words, scales, fmt):
    g, p, n, _ = words.shape
    if fmt == "e4m3":
        vals = np.ascontiguousarray(words).view(ml_dtypes.float8_e4m3fn).astype(np.float64)
    else:
        nib = np.empty((g, p, n, 4), np.uint8)
        nib[..., 0::2] = words & 0xF
        nib[..., 1::2] = words >> 4
        vals = E2M1[nib]
    vals = vals * np.repeat(np.exp2(scales.astype(np.float64) - 127.0), 8, axis=1)[..., None]
    return vals.transpose(0, 1, 3, 2).reshape(g * 512, n)


B, R, C, O, I = 256, 64, 8, 16, 512
EPS = 1e-8
ROUTING_ITERS = 3
FMT = "e4m3"


def squash(s):
    norm = np.sqrt((s * s).sum(axis=-1, keepdims=True))
    return norm / (1.0 + norm * norm + EPS) * s


def softmax(b, axis):
    e = np.exp(b - b.max(axis=axis, keepdims=True))
    return e / e.sum(axis=axis, keepdims=True)


def setup_inputs():
    s = mx_kscale(I)
    x = bf(np.random.standard_normal((B, R, I)) * s)
    stack = (np.random.standard_normal((R, C, O, I)) * (C / np.sqrt(R * O * I)) / s).swapaxes(-1, -2)
    words, scales = pack_weight(stack.reshape(-1, O), FMT)
    bias = bf(np.random.standard_normal((1, 1, C, O)) * 0.4 / np.sqrt(O))
    return {"x": x, "W_words": words, "W_scales": scales, "bias": bias}


def reference(x, W_words, W_scales, bias):
    xq = mxq(f64(x), 2, "e4m3")
    Wd = unpack_weight(W_words, W_scales, FMT).reshape(R, C, I, O)
    bias = f64(bias)
    u = xq.transpose(1, 0, 2) @ Wd.transpose(0, 2, 1, 3).reshape(R, I, C * O)
    u_hat = u.transpose(1, 0, 2).reshape(B, R, C, O)
    b_ij = np.zeros((B, R, C, 1))
    v_j = None
    for itr in range(ROUTING_ITERS):
        c_ij = softmax(b_ij, 2)
        s_j = (c_ij * u_hat).sum(axis=1, keepdims=True) + bias
        v_j = squash(s_j)
        if itr < ROUTING_ITERS - 1:
            a_ij = (u_hat * v_j).sum(axis=-1, keepdims=True)
            b_ij = b_ij + a_ij
    return v_j[:, 0]

@@ -1,0 +1,234 @@
+from contextlib import ExitStack
+
+import concourse.mybir as mybir
+from concourse.masks import make_identity
+
+F32 = mybir.dt.float32
+BF16 = mybir.dt.bfloat16
+I32 = mybir.dt.int32
+U32 = mybir.dt.uint32
+U8 = mybir.dt.uint8
+FP8X4 = mybir.dt.float8_e4m3fn_x4
+ACT = mybir.ActivationFunctionType
+ALU = mybir.AluOpType
+AX = mybir.AxisListType
+
+P = 128
+B, R, C, O, I = 256, 64, 8, 16, 512
+CO = C * O
+EPS = 1e-8
+ROUTING_ITERS = 3
+B_TILES = B // P
+ROUTES_PER_LOAD = 8
+ROUTES_PER_BANK = 4
+PAIR = 2
+C_PAIR = 2
+R_PART = 16
+SCALE_LOADS = 4
+WORD_ROUTES = 4
+
+FLOPS = 2 * B * R * C * O * I
+
+
+def load_weight(nc, keep, W_words, W_scales):
+    w_words = keep.tile([P, R, CO], U32, align_bytes=64)
+    w_scales = keep.tile([P, R * CO], U8, align_bytes=64)
+    nc.vector.memset(w_scales[:].bitcast(I32), 0)
+    scale_words = W_scales.bitcast(F32)
+    groups = R * C // SCALE_LOADS
+    for part in range(SCALE_LOADS):
+        for quadrant in range(4):
+            nc.gpsimd.dma_start(
+                out=w_scales[32 * quadrant : 32 * quadrant + 4, part * groups * O : (part + 1) * groups * O]
+                .bitcast(F32)
+                .rearrange("q (g w) -> q g w", w=O // 4),
+                in_=scale_words[part * groups : (part + 1) * groups, 4 * quadrant : 4 * quadrant + 4, :].rearrange(
+                    "g q w -> q g w"
+                ),
+            )
+    code_words = W_words.rearrange("g p n t -> g p (n t)").bitcast(I32).rearrange("g p w -> p g w")
+    for first in range(0, R, WORD_ROUTES):
+        nc.sync.dma_start(
+            out=w_words[:, first : first + WORD_ROUTES, :].bitcast(I32).rearrange("p r (c w) -> p (r c) w", w=O),
+            in_=code_words[:, first * C : (first + WORD_ROUTES) * C, :],
+        )
+    return w_words, w_scales
+
+
+def predictions(nc, pools, x_rows, ident, w_words, w_scales, bias_oc, u, s):
+    xin, stage, psum, psum_one = pools
+    route_sum = psum_one.tile([P, CO], F32)
+    for first in range(0, R, ROUTES_PER_LOAD):
+        x_sb = xin.tile([P, ROUTES_PER_LOAD, I], BF16)
+        nc.scalar.dma_start(out=x_sb[:], in_=x_rows[:, first : first + ROUTES_PER_LOAD, :])
+        x_words = x_sb[:].bitcast(F32)
+        grouped = stage.tile([P, ROUTES_PER_LOAD, P, 4], BF16, align_bytes=64)
+        grouped_words = grouped[:].bitcast(F32)
+        for pair in range(ROUTES_PER_LOAD // PAIR):
+            xt = psum.tile([P, PAIR, 2, P], F32)
+            for j in range(PAIR):
+                for h in range(2):
+                    nc.tensor.transpose(xt[:, j, h, :], x_words[:, pair * PAIR + j, h : I // 2 : 2], ident[:])
+            copy = nc.scalar.copy if pair % 2 == 0 else nc.vector.tensor_copy
+            copy(
+                out=grouped_words[:, pair * PAIR : (pair + 1) * PAIR, :, :],
+                in_=xt[:].rearrange("p j h b -> p j b h"),
+            )
+        x_codes = stage.tile([P, ROUTES_PER_LOAD * P], U32, align_bytes=64)
+        x_scales = stage.tile([P, ROUTES_PER_LOAD * P], U8, align_bytes=64)
+        nc.vector.quantize_mx(
+            out=x_codes[:].bitcast(FP8X4),
+            scales=x_scales[:],
+            in_=grouped[:].rearrange("p r b t -> p (r b t)"),
+        )
+        for bank in range(ROUTES_PER_LOAD // ROUTES_PER_BANK):
+            u_bank = psum.tile([P, ROUTES_PER_BANK, CO], F32)
+            for j in range(ROUTES_PER_BANK):
+                slot = bank * ROUTES_PER_BANK + j
+                r = first + slot
+                operands = dict(
+                    lhsT=x_codes[:, slot * P : (slot + 1) * P].bitcast(FP8X4),
+                    lhsT_scale=x_scales[:, slot * P : (slot + 1) * P],
+                    rhs=w_words[:, r, :].bitcast(FP8X4),
+                    rhs_scale=w_scales[:, r * CO : (r + 1) * CO],
+                )
+                nc.tensor.matmul_mx(out=u_bank[:, j, :], start=True, stop=True, **operands)
+                nc.tensor.matmul_mx(out=route_sum[:], start=(r == 0), stop=(r == R - 1), **operands)
+            r0 = first + bank * ROUTES_PER_BANK
+            nc.scalar.copy(
+                out=u[:, :, :, r0 : r0 + ROUTES_PER_BANK],
+                in_=u_bank[:].rearrange("p r (c o) -> p o c r", o=O),
+            )
+    nc.vector.scalar_tensor_tensor(
+        out=s[:],
+        in0=route_sum[:].rearrange("p (c o) -> p o c", o=O),
+        scalar=1.0 / C,
+        in1=bias_oc[:],
+        op0=ALU.mult,
+        op1=ALU.add,
+    )
+
+
+def squash_factor(nc, small, s, half):
+    squares = small.tile([P, O, C], F32)
+    nc.vector.tensor_tensor(out=squares[:], in0=s[:], in1=s[:], op=ALU.mult)
+    norm2 = small.tile([P, C], F32)
+    nc.vector.tensor_reduce(out=norm2[:], in_=squares[:].rearrange("p o c -> p c o"), axis=AX.X, op=ALU.add)
+    norm = small.tile([P, C], F32)
+    nc.gpsimd.tensor_tensor(out=norm[:], in0=norm2[:], in1=half[:], op=ALU.pow)
+    inverse = small.tile([P, C], F32)
+    nc.vector.tensor_scalar(out=inverse[:], in0=norm2[:], scalar1=1.0, scalar2=EPS, op0=ALU.add, op1=ALU.add)
+    nc.vector.reciprocal(out=inverse[:], in_=inverse[:])
+    factor = small.tile([P, C], F32)
+    nc.vector.tensor_tensor(out=factor[:], in0=norm[:], in1=inverse[:], op=ALU.mult)
+    return factor
+
+
+def add_transposed(nc, total, piece, ident, k, count):
+    nc.tensor.matmul(out=total, lhsT=piece, rhs=ident[:], is_transpose=True, start=(k == 0), stop=(k == count - 1))
+
+
+def routing(nc, pools, ident, half, u, s, bias_oc, out_rows):
+    small, state, work, psum_one = pools
+    v_sum = None
+    for iteration in range(1, ROUTING_ITERS):
+        factor = squash_factor(nc, small, s, half)
+        v = state.tile([P, O, C], F32)
+        nc.vector.tensor_tensor(
+            out=v[:], in0=s[:], in1=factor[:].unsqueeze(1).to_broadcast([P, O, C]), op=ALU.mult
+        )
+        if v_sum is not None:
+            nc.vector.tensor_tensor(out=v[:], in0=v[:], in1=v_sum[:], op=ALU.add)
+        v_sum = v
+        logits_t = psum_one.tile([P, C // C_PAIR, P], F32)
+        for pair in range(C // C_PAIR):
+            agreement = work.tile([P, O, C_PAIR, R], F32)
+            for o in range(O):
+                for j in range(C_PAIR):
+                    c = pair * C_PAIR + j
+                    nc.scalar.activation(
+                        out=agreement[:, o, j, :], in_=u[:, o, c, :], func=ACT.Copy, scale=v_sum[:, o, c : c + 1]
+                    )
+            for o in range(O):
+                add_transposed(nc, logits_t[:, pair, :], agreement[:, o, :, :].rearrange("p j r -> p (j r)"), ident, o, O)
+        logits_t_sb = small.tile([P, C // C_PAIR, P], F32)
+        nc.scalar.copy(out=logits_t_sb[:], in_=logits_t[:])
+        logits = psum_one.tile([P, C, R], F32, tag="back")
+        for pair in range(C // C_PAIR):
+            nc.tensor.transpose(
+                logits[:, pair * C_PAIR : (pair + 1) * C_PAIR, :].rearrange("p j r -> p (j r)"),
+                logits_t_sb[:, pair, :],
+                ident[:],
+            )
+        top = small.tile([P, R], F32)
+        nc.vector.tensor_reduce(out=top[:], in_=logits[:].rearrange("p c r -> p r c"), axis=AX.X, op=ALU.max)
+        coupling = small.tile([P, C, R], F32)
+        nc.vector.tensor_tensor(
+            out=coupling[:], in0=logits[:], in1=top[:].unsqueeze(1).to_broadcast([P, C, R]), op=ALU.subtract
+        )
+        nc.scalar.activation(out=coupling[:], in_=coupling[:], func=ACT.Exp)
+        total = small.tile([P, R], F32)
+        nc.vector.tensor_reduce(out=total[:], in_=coupling[:].rearrange("p c r -> p r c"), axis=AX.X, op=ALU.add)
+        nc.vector.reciprocal(out=total[:], in_=total[:])
+        nc.vector.tensor_tensor(
+            out=coupling[:], in0=coupling[:], in1=total[:].unsqueeze(1).to_broadcast([P, C, R]), op=ALU.mult
+        )
+        s_t = psum_one.tile([P, P], F32)
+        for first in range(0, R, R_PART):
+            weighted = work.tile([P, O, C, R_PART], F32)
+            nc.vector.tensor_tensor(
+                out=weighted[:],
+                in0=u[:, :, :, first : first + R_PART],
+                in1=coupling[:, :, first : first + R_PART].unsqueeze(1).to_broadcast([P, O, C, R_PART]),
+                op=ALU.mult,
+            )
+            for k in range(R_PART):
+                add_transposed(nc, s_t[:], weighted[:].rearrange("p o c r -> p (o c) r")[:, :, k], ident, first + k, R)
+        s_t_sb = small.tile([P, P], F32)
+        nc.vector.tensor_copy(out=s_t_sb[:], in_=s_t[:])
+        s_back = psum_one.tile([P, O, C], F32, tag="back")
+        nc.tensor.transpose(s_back[:].rearrange("p o c -> p (o c)"), s_t_sb[:], ident[:])
+        s = small.tile([P, O, C], F32)
+        nc.vector.tensor_tensor(out=s[:], in0=s_back[:], in1=bias_oc[:], op=ALU.add)
+    factor = squash_factor(nc, small, s, half)
+    v_out = small.tile([P, C, O], F32)
+    nc.vector.tensor_tensor(
+        out=v_out[:],
+        in0=s[:].rearrange("p o c -> p c o"),
+        in1=factor[:].unsqueeze(2).to_broadcast([P, C, O]),
+        op=ALU.mult,
+    )
+    nc.sync.dma_start(out=out_rows.rearrange("b c o -> b (c o)"), in_=v_out[:].rearrange("p c o -> p (c o)"))
+
+
+def tile_capsulelayer_e_kernel(tc, x, W_words, W_scales, bias, out):
+    nc = tc.nc
+    with ExitStack() as ctx:
+        keep = ctx.enter_context(tc.tile_pool(name="keep", bufs=1))
+        xin = ctx.enter_context(tc.tile_pool(name="xin", bufs=3))
+        stage = ctx.enter_context(tc.tile_pool(name="stage", bufs=2))
+        small = ctx.enter_context(tc.tile_pool(name="small", bufs=2))
+        state = ctx.enter_context(tc.tile_pool(name="state", bufs=(ROUTING_ITERS - 1) * B_TILES))
+        work = ctx.enter_context(tc.tile_pool(name="work", bufs=3))
+        psum = ctx.enter_context(tc.psum_pool(name="psum", bufs=2))
+        psum_one = ctx.enter_context(tc.psum_pool(name="psum_one", bufs=1))
+
+        ident = keep.tile([P, P], F32)
+        make_identity(nc, ident[:])
+        half = keep.tile([P, C], F32)
+        nc.gpsimd.memset(half[:], 0.5)
+        w_words, w_scales = load_weight(nc, keep, W_words, W_scales)
+        bias_rows = keep.tile([P, CO], BF16)
+        nc.sync.dma_start(out=bias_rows[:], in_=bias.rearrange("a b c o -> (a b c o)").partition_broadcast(P))
+        bias_oc = keep.tile([P, O, C], F32)
+        nc.vector.tensor_copy(out=bias_oc[:], in_=bias_rows[:].rearrange("p (c o) -> p o c", o=O))
+
+        batch_tiles = []
+        for bt in range(B_TILES):
+            u = keep.tile([P, O, C, R], F32, name="u%d" % bt)
+            s = keep.tile([P, O, C], F32, name="s%d" % bt)
+            rows = slice(bt * P, (bt + 1) * P)
+            predictions(nc, (xin, stage, psum, psum_one), x[rows], ident, w_words, w_scales, bias_oc, u, s)
+            batch_tiles.append((u, s, rows))
+        for u, s, rows in batch_tiles:
+            routing(nc, (small, state, work, psum_one), ident, half, u, s, bias_oc, out[rows])

@@ -22,8 +22,7 @@ B_TILES = B // P
 ROUTES_PER_LOAD = 8
 ROUTES_PER_BANK = 4
 PAIR = 2
-C_PAIR = 2
-R_PART = 16
+O_PART = 4
 SCALE_LOADS = 4
 WORD_ROUTES = 4
 
@@ -124,12 +123,8 @@ def squash_factor(nc, small, s, half):
     return factor
 
 
-def add_transposed(nc, total, piece, ident, k, count):
-    nc.tensor.matmul(out=total, lhsT=piece, rhs=ident[:], is_transpose=True, start=(k == 0), stop=(k == count - 1))
-
-
-def routing(nc, pools, ident, half, u, s, bias_oc, out_rows):
-    small, state, work, psum_one = pools
+def routing(nc, pools, half, u, s, bias_oc, out_rows):
+    small, state, work = pools
     v_sum = None
     for iteration in range(1, ROUTING_ITERS):
         factor = squash_factor(nc, small, s, half)
@@ -140,26 +135,20 @@ def routing(nc, pools, ident, half, u, s, bias_oc, out_rows):
         if v_sum is not None:
             nc.vector.tensor_tensor(out=v[:], in0=v[:], in1=v_sum[:], op=ALU.add)
         v_sum = v
-        logits_t = psum_one.tile([P, C // C_PAIR, P], F32)
-        for pair in range(C // C_PAIR):
-            agreement = work.tile([P, O, C_PAIR, R], F32)
-            for o in range(O):
-                for j in range(C_PAIR):
-                    c = pair * C_PAIR + j
-                    nc.scalar.activation(
-                        out=agreement[:, o, j, :], in_=u[:, o, c, :], func=ACT.Copy, scale=v_sum[:, o, c : c + 1]
+        logits = small.tile([P, C, R], F32)
+        for o in range(O):
+            for c in range(C):
+                if o == 0:
+                    nc.vector.tensor_scalar_mul(out=logits[:, c, :], in0=u[:, o, c, :], scalar1=v_sum[:, o, c : c + 1])
+                else:
+                    nc.vector.scalar_tensor_tensor(
+                        out=logits[:, c, :],
+                        in0=u[:, o, c, :],
+                        scalar=v_sum[:, o, c : c + 1],
+                        in1=logits[:, c, :],
+                        op0=ALU.mult,
+                        op1=ALU.add,
                     )
-            for o in range(O):
-                add_transposed(nc, logits_t[:, pair, :], agreement[:, o, :, :].rearrange("p j r -> p (j r)"), ident, o, O)
-        logits_t_sb = small.tile([P, C // C_PAIR, P], F32)
-        nc.scalar.copy(out=logits_t_sb[:], in_=logits_t[:])
-        logits = psum_one.tile([P, C, R], F32, tag="back")
-        for pair in range(C // C_PAIR):
-            nc.tensor.transpose(
-                logits[:, pair * C_PAIR : (pair + 1) * C_PAIR, :].rearrange("p j r -> p (j r)"),
-                logits_t_sb[:, pair, :],
-                ident[:],
-            )
         top = small.tile([P, R], F32)
         nc.vector.tensor_reduce(out=top[:], in_=logits[:].rearrange("p c r -> p r c"), axis=AX.X, op=ALU.max)
         coupling = small.tile([P, C, R], F32)
@@ -173,23 +162,17 @@ def routing(nc, pools, ident, half, u, s, bias_oc, out_rows):
         nc.vector.tensor_tensor(
             out=coupling[:], in0=coupling[:], in1=total[:].unsqueeze(1).to_broadcast([P, C, R]), op=ALU.mult
         )
-        s_t = psum_one.tile([P, P], F32)
-        for first in range(0, R, R_PART):
-            weighted = work.tile([P, O, C, R_PART], F32)
+        s = small.tile([P, O, C], F32)
+        for first in range(0, O, O_PART):
+            weighted = work.tile([P, O_PART, C, R], F32)
             nc.vector.tensor_tensor(
                 out=weighted[:],
-                in0=u[:, :, :, first : first + R_PART],
-                in1=coupling[:, :, first : first + R_PART].unsqueeze(1).to_broadcast([P, O, C, R_PART]),
+                in0=u[:, first : first + O_PART, :, :],
+                in1=coupling[:].unsqueeze(1).to_broadcast([P, O_PART, C, R]),
                 op=ALU.mult,
             )
-            for k in range(R_PART):
-                add_transposed(nc, s_t[:], weighted[:].rearrange("p o c r -> p (o c) r")[:, :, k], ident, first + k, R)
-        s_t_sb = small.tile([P, P], F32)
-        nc.vector.tensor_copy(out=s_t_sb[:], in_=s_t[:])
-        s_back = psum_one.tile([P, O, C], F32, tag="back")
-        nc.tensor.transpose(s_back[:].rearrange("p o c -> p (o c)"), s_t_sb[:], ident[:])
-        s = small.tile([P, O, C], F32)
-        nc.vector.tensor_tensor(out=s[:], in0=s_back[:], in1=bias_oc[:], op=ALU.add)
+            nc.vector.tensor_reduce(out=s[:, first : first + O_PART, :], in_=weighted[:], axis=AX.X, op=ALU.add)
+        nc.vector.tensor_tensor(out=s[:], in0=s[:], in1=bias_oc[:], op=ALU.add)
     factor = squash_factor(nc, small, s, half)
     v_out = small.tile([P, C, O], F32)
     nc.vector.tensor_tensor(
@@ -231,4 +214,4 @@ def tile_capsulelayer_e_kernel(tc, x, W_words, W_scales, bias, out):
             predictions(nc, (xin, stage, psum, psum_one), x[rows], ident, w_words, w_scales, bias_oc, u, s)
             batch_tiles.append((u, s, rows))
         for u, s, rows in batch_tiles:
-            routing(nc, (small, state, work, psum_one), ident, half, u, s, bias_oc, out[rows])
+            routing(nc, (small, state, work), half, u, s, bias_oc, out[rows])

@@ -23,89 +23,123 @@ ROUTES_PER_LOAD = 8
 ROUTES_PER_BANK = 4
 PAIR = 2
 O_PART = 4
-SCALE_LOADS = 4
+C_PAIR = 2
+SCALE_ROUTES = 16
+PREFETCH = 3
 WORD_ROUTES = 4
 
 FLOPS = 2 * B * R * C * O * I
 
 
-def load_weight(nc, keep, W_words, W_scales):
-    w_words = keep.tile([P, R, CO], U32, align_bytes=64)
-    w_scales = keep.tile([P, R * CO], U8, align_bytes=64)
-    nc.vector.memset(w_scales[:].bitcast(I32), 0)
-    scale_words = W_scales.bitcast(F32)
-    groups = R * C // SCALE_LOADS
-    for part in range(SCALE_LOADS):
+def load_weight_routes(nc, W_words, W_scales, w_words, w_scales, first):
+    if first % SCALE_ROUTES == 0:
+        scale_words = W_scales.bitcast(I32)
         for quadrant in range(4):
-            nc.gpsimd.dma_start(
-                out=w_scales[32 * quadrant : 32 * quadrant + 4, part * groups * O : (part + 1) * groups * O]
-                .bitcast(F32)
+            nc.sync.dma_start(
+                out=w_scales[32 * quadrant : 32 * quadrant + 4, first * CO : (first + SCALE_ROUTES) * CO]
+                .bitcast(I32)
                 .rearrange("q (g w) -> q g w", w=O // 4),
-                in_=scale_words[part * groups : (part + 1) * groups, 4 * quadrant : 4 * quadrant + 4, :].rearrange(
+                in_=scale_words[first * C : (first + SCALE_ROUTES) * C, 4 * quadrant : 4 * quadrant + 4, :].rearrange(
                     "g q w -> q g w"
                 ),
             )
     code_words = W_words.rearrange("g p n t -> g p (n t)").bitcast(I32).rearrange("g p w -> p g w")
-    for first in range(0, R, WORD_ROUTES):
+    for j in range(0, ROUTES_PER_LOAD, WORD_ROUTES):
         nc.sync.dma_start(
-            out=w_words[:, first : first + WORD_ROUTES, :].bitcast(I32).rearrange("p r (c w) -> p (r c) w", w=O),
-            in_=code_words[:, first * C : (first + WORD_ROUTES) * C, :],
+            out=w_words[:, j : j + WORD_ROUTES, :].bitcast(I32).rearrange("p r (c w) -> p (r c) w", w=O),
+            in_=code_words[:, (first + j) * C : (first + j + WORD_ROUTES) * C, :],
         )
-    return w_words, w_scales
 
 
-def predictions(nc, pools, x_rows, ident, w_words, w_scales, bias_oc, u, s):
-    xin, stage, psum, psum_one = pools
-    route_sum = psum_one.tile([P, CO], F32)
-    for first in range(0, R, ROUTES_PER_LOAD):
-        x_sb = xin.tile([P, ROUTES_PER_LOAD, I], BF16)
-        nc.scalar.dma_start(out=x_sb[:], in_=x_rows[:, first : first + ROUTES_PER_LOAD, :])
-        x_words = x_sb[:].bitcast(F32)
-        grouped = stage.tile([P, ROUTES_PER_LOAD, P, 4], BF16, align_bytes=64)
-        grouped_words = grouped[:].bitcast(F32)
-        for pair in range(ROUTES_PER_LOAD // PAIR):
-            xt = psum.tile([P, PAIR, 2, P], F32)
-            for j in range(PAIR):
-                for h in range(2):
-                    nc.tensor.transpose(xt[:, j, h, :], x_words[:, pair * PAIR + j, h : I // 2 : 2], ident[:])
-            copy = nc.scalar.copy if pair % 2 == 0 else nc.vector.tensor_copy
-            copy(
-                out=grouped_words[:, pair * PAIR : (pair + 1) * PAIR, :, :],
-                in_=xt[:].rearrange("p j h b -> p j b h"),
-            )
-        x_codes = stage.tile([P, ROUTES_PER_LOAD * P], U32, align_bytes=64)
-        x_scales = stage.tile([P, ROUTES_PER_LOAD * P], U8, align_bytes=64)
-        nc.vector.quantize_mx(
-            out=x_codes[:].bitcast(FP8X4),
-            scales=x_scales[:],
-            in_=grouped[:].rearrange("p r b t -> p (r b t)"),
+def transpose_routes(nc, pools, x_sb, ident):
+    stage, psum = pools
+    x_words = x_sb[:].bitcast(F32)
+    grouped = stage.tile([P, ROUTES_PER_LOAD, P, 4], BF16, align_bytes=64)
+    grouped_words = grouped[:].bitcast(F32)
+    for pair in range(ROUTES_PER_LOAD // PAIR):
+        xt = psum.tile([P, PAIR, 2, P], F32)
+        for j in range(PAIR):
+            for h in range(2):
+                nc.tensor.transpose(xt[:, j, h, :], x_words[:, pair * PAIR + j, h : I // 2 : 2], ident[:])
+        nc.scalar.copy(
+            out=grouped_words[:, pair * PAIR : (pair + 1) * PAIR, :, :],
+            in_=xt[:].rearrange("p j h b -> p j b h"),
         )
-        for bank in range(ROUTES_PER_LOAD // ROUTES_PER_BANK):
-            u_bank = psum.tile([P, ROUTES_PER_BANK, CO], F32)
-            for j in range(ROUTES_PER_BANK):
-                slot = bank * ROUTES_PER_BANK + j
-                r = first + slot
-                operands = dict(
-                    lhsT=x_codes[:, slot * P : (slot + 1) * P].bitcast(FP8X4),
-                    lhsT_scale=x_scales[:, slot * P : (slot + 1) * P],
-                    rhs=w_words[:, r, :].bitcast(FP8X4),
-                    rhs_scale=w_scales[:, r * CO : (r + 1) * CO],
-                )
-                nc.tensor.matmul_mx(out=u_bank[:, j, :], start=True, stop=True, **operands)
-                nc.tensor.matmul_mx(out=route_sum[:], start=(r == 0), stop=(r == R - 1), **operands)
-            r0 = first + bank * ROUTES_PER_BANK
-            nc.scalar.copy(
-                out=u[:, :, :, r0 : r0 + ROUTES_PER_BANK],
-                in_=u_bank[:].rearrange("p r (c o) -> p o c r", o=O),
-            )
-    nc.vector.scalar_tensor_tensor(
-        out=s[:],
-        in0=route_sum[:].rearrange("p (c o) -> p o c", o=O),
-        scalar=1.0 / C,
-        in1=bias_oc[:],
-        op0=ALU.mult,
-        op1=ALU.add,
+    return grouped
+
+
+def quantise_routes(nc, stage, grouped):
+    x_codes = stage.tile([P, ROUTES_PER_LOAD * P], U32, align_bytes=64)
+    x_scales = stage.tile([P, ROUTES_PER_LOAD * P], U8, align_bytes=64)
+    nc.vector.quantize_mx(
+        out=x_codes[:].bitcast(FP8X4),
+        scales=x_scales[:],
+        in_=grouped[:].rearrange("p r b t -> p (r b t)"),
     )
+    return x_codes, x_scales
+
+
+def multiply_routes(nc, psum, first, x_codes, x_scales, w_words, w_scales, u, route_sum):
+    for bank in range(ROUTES_PER_LOAD // ROUTES_PER_BANK):
+        u_bank = psum.tile([P, ROUTES_PER_BANK, CO], F32)
+        for j in range(ROUTES_PER_BANK):
+            slot = bank * ROUTES_PER_BANK + j
+            r = first + slot
+            operands = dict(
+                lhsT=x_codes[:, slot * P : (slot + 1) * P].bitcast(FP8X4),
+                lhsT_scale=x_scales[:, slot * P : (slot + 1) * P],
+                rhs=w_words[:, slot, :].bitcast(FP8X4),
+                rhs_scale=w_scales[:, r * CO : (r + 1) * CO],
+            )
+            nc.tensor.matmul_mx(out=u_bank[:, j, :], start=True, stop=True, **operands)
+            nc.tensor.matmul_mx(out=route_sum[:], start=(r == 0), stop=(r == R - 1), **operands)
+        r0 = first + bank * ROUTES_PER_BANK
+        nc.scalar.copy(
+            out=u[:, :, :, r0 : r0 + ROUTES_PER_BANK],
+            in_=u_bank[:].rearrange("p r (c o) -> p o c r", o=O),
+        )
+
+
+def predictions(nc, pools, x, W_words, W_scales, ident, bias_oc, batch_tiles):
+    keep, win, xin, stage, psum, psum_one = pools
+    w_scales = keep.tile([P, R * CO], U8, align_bytes=64)
+    nc.vector.memset(w_scales[:].bitcast(I32), 0)
+    steps = [(bt, first) for first in range(0, R, ROUTES_PER_LOAD) for bt in range(B_TILES)]
+    weights = {}
+    loaded = {}
+    grouped = {}
+    quantised = {}
+    sum_banks = {}
+    for k in range(-PREFETCH, len(steps) + 2):
+        if k + PREFETCH < len(steps):
+            bt, first = steps[k + PREFETCH]
+            if bt == 0:
+                w_words = win.tile([P, ROUTES_PER_LOAD, CO], U32, align_bytes=64)
+                load_weight_routes(nc, W_words, W_scales, w_words, w_scales, first)
+                weights[first] = w_words
+            x_sb = xin.tile([P, ROUTES_PER_LOAD, I], BF16)
+            nc.sync.dma_start(out=x_sb[:], in_=x[bt * P : (bt + 1) * P, first : first + ROUTES_PER_LOAD, :])
+            loaded[k + PREFETCH] = x_sb
+        if 0 <= k < len(steps):
+            grouped[k] = transpose_routes(nc, (stage, psum), loaded[k], ident)
+        if 1 <= k <= len(steps):
+            quantised[k - 1] = quantise_routes(nc, stage, grouped[k - 1])
+        if k >= 2:
+            bt, first = steps[k - 2]
+            u, s = batch_tiles[bt]["u"], batch_tiles[bt]["s"]
+            if first == 0:
+                sum_banks[bt] = psum_one.tile([P, CO], F32, name="route_sum%d" % bt)
+            x_codes, x_scales = quantised[k - 2]
+            multiply_routes(nc, psum, first, x_codes, x_scales, weights[first], w_scales, u, sum_banks[bt])
+            if first + ROUTES_PER_LOAD == R:
+                nc.vector.scalar_tensor_tensor(
+                    out=s[:],
+                    in0=sum_banks[bt][:].rearrange("p (c o) -> p o c", o=O),
+                    scalar=1.0 / C,
+                    in1=bias_oc[:],
+                    op0=ALU.mult,
+                    op1=ALU.add,
+                )
 
 
 def squash_factor(nc, small, s, half):
@@ -123,56 +157,89 @@ def squash_factor(nc, small, s, half):
     return factor
 
 
-def routing(nc, pools, half, u, s, bias_oc, out_rows):
-    small, state, work = pools
-    v_sum = None
-    for iteration in range(1, ROUTING_ITERS):
-        factor = squash_factor(nc, small, s, half)
-        v = state.tile([P, O, C], F32)
-        nc.vector.tensor_tensor(
-            out=v[:], in0=s[:], in1=factor[:].unsqueeze(1).to_broadcast([P, O, C]), op=ALU.mult
-        )
-        if v_sum is not None:
-            nc.vector.tensor_tensor(out=v[:], in0=v[:], in1=v_sum[:], op=ALU.add)
-        v_sum = v
-        logits = small.tile([P, C, R], F32)
+def squash(nc, pools, tile_state, half):
+    small, state = pools
+    s = tile_state["s"]
+    factor = squash_factor(nc, small, s, half)
+    v = state.tile([P, O, C], F32)
+    nc.vector.tensor_tensor(out=v[:], in0=s[:], in1=factor[:].unsqueeze(1).to_broadcast([P, O, C]), op=ALU.mult)
+    if "v_sum" in tile_state:
+        nc.vector.tensor_tensor(out=v[:], in0=v[:], in1=tile_state["v_sum"][:], op=ALU.add)
+    tile_state["v_sum"] = v
+
+
+def agreement(nc, pools, tile_state, ident):
+    small, work, psum = pools
+    u = tile_state["u"]
+    v_sum = tile_state["v_sum"]
+    logits_t = psum.tile([P, C // C_PAIR, P], F32)
+    for pair in range(C // C_PAIR):
+        products = work.tile([P, O, C_PAIR, R], F32)
         for o in range(O):
-            for c in range(C):
-                if o == 0:
-                    nc.vector.tensor_scalar_mul(out=logits[:, c, :], in0=u[:, o, c, :], scalar1=v_sum[:, o, c : c + 1])
-                else:
-                    nc.vector.scalar_tensor_tensor(
-                        out=logits[:, c, :],
-                        in0=u[:, o, c, :],
-                        scalar=v_sum[:, o, c : c + 1],
-                        in1=logits[:, c, :],
-                        op0=ALU.mult,
-                        op1=ALU.add,
-                    )
-        top = small.tile([P, R], F32)
-        nc.vector.tensor_reduce(out=top[:], in_=logits[:].rearrange("p c r -> p r c"), axis=AX.X, op=ALU.max)
-        coupling = small.tile([P, C, R], F32)
-        nc.vector.tensor_tensor(
-            out=coupling[:], in0=logits[:], in1=top[:].unsqueeze(1).to_broadcast([P, C, R]), op=ALU.subtract
-        )
-        nc.scalar.activation(out=coupling[:], in_=coupling[:], func=ACT.Exp)
-        total = small.tile([P, R], F32)
-        nc.vector.tensor_reduce(out=total[:], in_=coupling[:].rearrange("p c r -> p r c"), axis=AX.X, op=ALU.add)
-        nc.vector.reciprocal(out=total[:], in_=total[:])
-        nc.vector.tensor_tensor(
-            out=coupling[:], in0=coupling[:], in1=total[:].unsqueeze(1).to_broadcast([P, C, R]), op=ALU.mult
-        )
-        s = small.tile([P, O, C], F32)
-        for first in range(0, O, O_PART):
-            weighted = work.tile([P, O_PART, C, R], F32)
-            nc.vector.tensor_tensor(
-                out=weighted[:],
-                in0=u[:, first : first + O_PART, :, :],
-                in1=coupling[:].unsqueeze(1).to_broadcast([P, O_PART, C, R]),
-                op=ALU.mult,
+            for j in range(C_PAIR):
+                c = pair * C_PAIR + j
+                nc.scalar.activation(
+                    out=products[:, o, j, :], in_=u[:, o, c, :], func=ACT.Copy, scale=v_sum[:, o, c : c + 1]
+                )
+        for o in range(O):
+            nc.tensor.matmul(
+                out=logits_t[:, pair, :],
+                lhsT=products[:, o, :, :].rearrange("p j r -> p (j r)"),
+                rhs=ident[:],
+                is_transpose=True,
+                start=(o == 0),
+                stop=(o == O - 1),
             )
-            nc.vector.tensor_reduce(out=s[:, first : first + O_PART, :], in_=weighted[:], axis=AX.X, op=ALU.add)
-        nc.vector.tensor_tensor(out=s[:], in0=s[:], in1=bias_oc[:], op=ALU.add)
+    logits_t_sb = small.tile([P, C // C_PAIR, P], F32)
+    nc.scalar.copy(out=logits_t_sb[:], in_=logits_t[:])
+    logits = psum.tile([P, C, R], F32)
+    for pair in range(C // C_PAIR):
+        nc.tensor.transpose(
+            logits[:, pair * C_PAIR : (pair + 1) * C_PAIR, :].rearrange("p j r -> p (j r)"),
+            logits_t_sb[:, pair, :],
+            ident[:],
+        )
+    tile_state["logits"] = logits
+
+
+def exponentials(nc, small, tile_state):
+    logits = tile_state["logits"]
+    top = small.tile([P, R], F32)
+    nc.vector.tensor_reduce(out=top[:], in_=logits[:].rearrange("p c r -> p r c"), axis=AX.X, op=ALU.max)
+    coupling = small.tile([P, C, R], F32)
+    nc.vector.tensor_tensor(
+        out=coupling[:], in0=logits[:], in1=top[:].unsqueeze(1).to_broadcast([P, C, R]), op=ALU.subtract
+    )
+    nc.scalar.activation(out=coupling[:], in_=coupling[:], func=ACT.Exp)
+    tile_state["coupling"] = coupling
+
+
+def route_sums(nc, pools, tile_state, bias_oc):
+    small, work = pools
+    u = tile_state["u"]
+    coupling = tile_state["coupling"]
+    total = small.tile([P, R], F32)
+    nc.vector.tensor_reduce(out=total[:], in_=coupling[:].rearrange("p c r -> p r c"), axis=AX.X, op=ALU.add)
+    nc.vector.reciprocal(out=total[:], in_=total[:])
+    nc.vector.tensor_tensor(
+        out=coupling[:], in0=coupling[:], in1=total[:].unsqueeze(1).to_broadcast([P, C, R]), op=ALU.mult
+    )
+    s = small.tile([P, O, C], F32)
+    for first in range(0, O, O_PART):
+        weighted = work.tile([P, O_PART, C, R], F32)
+        nc.vector.tensor_tensor(
+            out=weighted[:],
+            in0=u[:, first : first + O_PART, :, :],
+            in1=coupling[:].unsqueeze(1).to_broadcast([P, O_PART, C, R]),
+            op=ALU.mult,
+        )
+        nc.vector.tensor_reduce(out=s[:, first : first + O_PART, :], in_=weighted[:], axis=AX.X, op=ALU.add)
+    nc.vector.tensor_tensor(out=s[:], in0=s[:], in1=bias_oc[:], op=ALU.add)
+    tile_state["s"] = s
+
+
+def store_output(nc, small, tile_state, half, out_rows):
+    s = tile_state["s"]
     factor = squash_factor(nc, small, s, half)
     v_out = small.tile([P, C, O], F32)
     nc.vector.tensor_tensor(
@@ -184,34 +251,52 @@ def routing(nc, pools, half, u, s, bias_oc, out_rows):
     nc.sync.dma_start(out=out_rows.rearrange("b c o -> b (c o)"), in_=v_out[:].rearrange("p c o -> p (c o)"))
 
 
+def routing(nc, pools, ident, half, bias_oc, tile_states, out):
+    small, state, work, psum = pools
+    turns = [(iteration, bt) for iteration in range(1, ROUTING_ITERS) for bt in range(B_TILES)]
+    for bt in range(B_TILES):
+        squash(nc, (small, state), tile_states[bt], half)
+    agreement(nc, (small, work, psum), tile_states[0], ident)
+    for k, (iteration, bt) in enumerate(turns):
+        exponentials(nc, small, tile_states[bt])
+        if k + 1 < len(turns):
+            agreement(nc, (small, work, psum), tile_states[turns[k + 1][1]], ident)
+        route_sums(nc, (small, work), tile_states[bt], bias_oc)
+        if iteration + 1 < ROUTING_ITERS:
+            squash(nc, (small, state), tile_states[bt], half)
+        else:
+            store_output(nc, small, tile_states[bt], half, out[bt * P : (bt + 1) * P])
+
+
 def tile_capsulelayer_e_kernel(tc, x, W_words, W_scales, bias, out):
     nc = tc.nc
-    with ExitStack() as ctx:
-        keep = ctx.enter_context(tc.tile_pool(name="keep", bufs=1))
-        xin = ctx.enter_context(tc.tile_pool(name="xin", bufs=3))
-        stage = ctx.enter_context(tc.tile_pool(name="stage", bufs=2))
-        small = ctx.enter_context(tc.tile_pool(name="small", bufs=2))
-        state = ctx.enter_context(tc.tile_pool(name="state", bufs=(ROUTING_ITERS - 1) * B_TILES))
-        work = ctx.enter_context(tc.tile_pool(name="work", bufs=3))
-        psum = ctx.enter_context(tc.psum_pool(name="psum", bufs=2))
-        psum_one = ctx.enter_context(tc.psum_pool(name="psum_one", bufs=1))
-
+    with tc.tile_pool(name="keep", bufs=1) as keep:
         ident = keep.tile([P, P], F32)
         make_identity(nc, ident[:])
         half = keep.tile([P, C], F32)
         nc.gpsimd.memset(half[:], 0.5)
-        w_words, w_scales = load_weight(nc, keep, W_words, W_scales)
         bias_rows = keep.tile([P, CO], BF16)
         nc.sync.dma_start(out=bias_rows[:], in_=bias.rearrange("a b c o -> (a b c o)").partition_broadcast(P))
         bias_oc = keep.tile([P, O, C], F32)
         nc.vector.tensor_copy(out=bias_oc[:], in_=bias_rows[:].rearrange("p (c o) -> p o c", o=O))
-
-        batch_tiles = []
+        tile_states = []
         for bt in range(B_TILES):
             u = keep.tile([P, O, C, R], F32, name="u%d" % bt)
             s = keep.tile([P, O, C], F32, name="s%d" % bt)
-            rows = slice(bt * P, (bt + 1) * P)
-            predictions(nc, (xin, stage, psum, psum_one), x[rows], ident, w_words, w_scales, bias_oc, u, s)
-            batch_tiles.append((u, s, rows))
-        for u, s, rows in batch_tiles:
-            routing(nc, (small, state, work), half, u, s, bias_oc, out[rows])
+            tile_states.append({"u": u, "s": s})
+
+        with ExitStack() as ctx:
+            win = ctx.enter_context(tc.tile_pool(name="win", bufs=4))
+            xin = ctx.enter_context(tc.tile_pool(name="xin", bufs=PREFETCH + 1))
+            stage = ctx.enter_context(tc.tile_pool(name="stage", bufs=2))
+            psum = ctx.enter_context(tc.psum_pool(name="psum", bufs=2))
+            psum_one = ctx.enter_context(tc.psum_pool(name="psum_one", bufs=1))
+            pools = (keep, win, xin, stage, psum, psum_one)
+            predictions(nc, pools, x, W_words, W_scales, ident, bias_oc, tile_states)
+
+        with ExitStack() as ctx:
+            small = ctx.enter_context(tc.tile_pool(name="small", bufs=2))
+            state = ctx.enter_context(tc.tile_pool(name="state", bufs=(ROUTING_ITERS - 1) * B_TILES))
+            work = ctx.enter_context(tc.tile_pool(name="work", bufs=3))
+            psum = ctx.enter_context(tc.psum_pool(name="psum_routing", bufs=2))
+            routing(nc, (small, state, work, psum), ident, half, bias_oc, tile_states, out)

@@ -24,25 +24,45 @@ ROUTES_PER_BANK = 4
 PAIR = 2
 O_PART = 4
 C_PAIR = 2
-SCALE_ROUTES = 16
+PLANES = 4
+PLANE_ROUTES = R // PLANES
+GROUP_WORDS = 16 * O // 4
+PLANE_WORDS = PLANE_ROUTES * C * GROUP_WORDS
+WINDOW_WORDS = PLANE_WORDS - 48
 PREFETCH = 3
 WORD_ROUTES = 4
 
 FLOPS = 2 * B * R * C * O * I
 
 
-def load_weight_routes(nc, W_words, W_scales, w_words, w_scales, first):
-    if first % SCALE_ROUTES == 0:
-        scale_words = W_scales.bitcast(I32)
+def load_scale_runs(nc, raw_pool, W_scales):
+    raw = raw_pool.tile([P, PLANE_WORDS], I32)
+    all_words = W_scales.rearrange("g q n -> (g q n)").bitcast(I32)
+    for k in range(4):
         for quadrant in range(4):
-            nc.sync.dma_start(
-                out=w_scales[32 * quadrant : 32 * quadrant + 4, first * CO : (first + SCALE_ROUTES) * CO]
-                .bitcast(I32)
-                .rearrange("q (g w) -> q g w", w=O // 4),
-                in_=scale_words[first * C : (first + SCALE_ROUTES) * C, 4 * quadrant : 4 * quadrant + 4, :].rearrange(
-                    "g q w -> q g w"
-                ),
-            )
+            for j in range(PLANES):
+                partition = 32 * quadrant + 4 * j + k
+                start = j * PLANE_WORDS + 4 * k + 12 * quadrant
+                nc.sync.dma_start(
+                    out=raw[partition : partition + 1, 0:WINDOW_WORDS].rearrange("o (a b) -> o a b", a=16),
+                    in_=all_words[start : start + WINDOW_WORDS].rearrange("(a b) -> a b", a=16).unsqueeze(0),
+                )
+    return raw
+
+
+def pick_scale_rows(nc, keep, raw):
+    w_scales = keep.tile([P, PLANE_ROUTES * CO], U8, align_bytes=64)
+    nc.vector.memset(w_scales[:].bitcast(I32), 0)
+    for quadrant in range(4):
+        rows = slice(32 * quadrant, 32 * quadrant + 4 * PLANES)
+        nc.vector.tensor_copy(
+            out=w_scales[rows, :].bitcast(I32).rearrange("p (g w) -> p g w", w=O // 4),
+            in_=raw[rows, :].rearrange("p (g w) -> p g w", w=GROUP_WORDS)[:, :, 4 * quadrant : 4 * quadrant + O // 4],
+        )
+    return w_scales
+
+
+def load_weight_routes(nc, W_words, w_words, first):
     code_words = W_words.rearrange("g p n t -> g p (n t)").bitcast(I32).rearrange("g p w -> p g w")
     for j in range(0, ROUTES_PER_LOAD, WORD_ROUTES):
         nc.sync.dma_start(
@@ -51,7 +71,7 @@ def load_weight_routes(nc, W_words, W_scales, w_words, w_scales, first):
         )
 
 
-def transpose_routes(nc, pools, x_sb, ident):
+def transpose_routes(nc, pools, copy, x_sb, ident):
     stage, psum = pools
     x_words = x_sb[:].bitcast(F32)
     grouped = stage.tile([P, ROUTES_PER_LOAD, P, 4], BF16, align_bytes=64)
@@ -61,7 +81,7 @@ def transpose_routes(nc, pools, x_sb, ident):
         for j in range(PAIR):
             for h in range(2):
                 nc.tensor.transpose(xt[:, j, h, :], x_words[:, pair * PAIR + j, h : I // 2 : 2], ident[:])
-        nc.scalar.copy(
+        copy(
             out=grouped_words[:, pair * PAIR : (pair + 1) * PAIR, :, :],
             in_=xt[:].rearrange("p j h b -> p j b h"),
         )
@@ -79,7 +99,7 @@ def quantise_routes(nc, stage, grouped):
     return x_codes, x_scales
 
 
-def multiply_routes(nc, psum, first, x_codes, x_scales, w_words, w_scales, u, route_sum):
+def multiply_routes(nc, psum, copy, first, x_codes, x_scales, w_words, w_scales, u, route_sum):
     for bank in range(ROUTES_PER_LOAD // ROUTES_PER_BANK):
         u_bank = psum.tile([P, ROUTES_PER_BANK, CO], F32)
         for j in range(ROUTES_PER_BANK):
@@ -89,21 +109,20 @@ def multiply_routes(nc, psum, first, x_codes, x_scales, w_words, w_scales, u, ro
                 lhsT=x_codes[:, slot * P : (slot + 1) * P].bitcast(FP8X4),
                 lhsT_scale=x_scales[:, slot * P : (slot + 1) * P],
                 rhs=w_words[:, slot, :].bitcast(FP8X4),
-                rhs_scale=w_scales[:, r * CO : (r + 1) * CO],
+                rhs_scale=w_scales[4 * (r // PLANE_ROUTES) : P, (r % PLANE_ROUTES) * CO : (r % PLANE_ROUTES + 1) * CO],
             )
             nc.tensor.matmul_mx(out=u_bank[:, j, :], start=True, stop=True, **operands)
             nc.tensor.matmul_mx(out=route_sum[:], start=(r == 0), stop=(r == R - 1), **operands)
         r0 = first + bank * ROUTES_PER_BANK
-        nc.scalar.copy(
+        copy(
             out=u[:, :, :, r0 : r0 + ROUTES_PER_BANK],
             in_=u_bank[:].rearrange("p r (c o) -> p o c r", o=O),
         )
 
 
 def predictions(nc, pools, x, W_words, W_scales, ident, bias_oc, batch_tiles):
-    keep, win, xin, stage, psum, psum_one = pools
-    w_scales = keep.tile([P, R * CO], U8, align_bytes=64)
-    nc.vector.memset(w_scales[:].bitcast(I32), 0)
+    keep, raw_pool, win, xin, stage, psum, psum_one = pools
+    copies = [nc.scalar.copy, nc.vector.tensor_copy]
     steps = [(bt, first) for first in range(0, R, ROUTES_PER_LOAD) for bt in range(B_TILES)]
     weights = {}
     loaded = {}
@@ -115,22 +134,26 @@ def predictions(nc, pools, x, W_words, W_scales, ident, bias_oc, batch_tiles):
             bt, first = steps[k + PREFETCH]
             if bt == 0:
                 w_words = win.tile([P, ROUTES_PER_LOAD, CO], U32, align_bytes=64)
-                load_weight_routes(nc, W_words, W_scales, w_words, w_scales, first)
+                load_weight_routes(nc, W_words, w_words, first)
                 weights[first] = w_words
             x_sb = xin.tile([P, ROUTES_PER_LOAD, I], BF16)
             nc.sync.dma_start(out=x_sb[:], in_=x[bt * P : (bt + 1) * P, first : first + ROUTES_PER_LOAD, :])
             loaded[k + PREFETCH] = x_sb
+        if k == 0:
+            raw = load_scale_runs(nc, raw_pool, W_scales)
         if 0 <= k < len(steps):
-            grouped[k] = transpose_routes(nc, (stage, psum), loaded[k], ident)
+            grouped[k] = transpose_routes(nc, (stage, psum), copies[steps[k][0]], loaded[k], ident)
         if 1 <= k <= len(steps):
             quantised[k - 1] = quantise_routes(nc, stage, grouped[k - 1])
+        if k == 2:
+            w_scales = pick_scale_rows(nc, keep, raw)
         if k >= 2:
             bt, first = steps[k - 2]
             u, s = batch_tiles[bt]["u"], batch_tiles[bt]["s"]
             if first == 0:
                 sum_banks[bt] = psum_one.tile([P, CO], F32, name="route_sum%d" % bt)
             x_codes, x_scales = quantised[k - 2]
-            multiply_routes(nc, psum, first, x_codes, x_scales, weights[first], w_scales, u, sum_banks[bt])
+            multiply_routes(nc, psum, copies[bt], first, x_codes, x_scales, weights[first], w_scales, u, sum_banks[bt])
             if first + ROUTES_PER_LOAD == R:
                 nc.vector.scalar_tensor_tensor(
                     out=s[:],
@@ -286,12 +309,13 @@ def tile_capsulelayer_e_kernel(tc, x, W_words, W_scales, bias, out):
             tile_states.append({"u": u, "s": s})
 
         with ExitStack() as ctx:
+            raw_pool = ctx.enter_context(tc.tile_pool(name="raw", bufs=1))
             win = ctx.enter_context(tc.tile_pool(name="win", bufs=4))
             xin = ctx.enter_context(tc.tile_pool(name="xin", bufs=PREFETCH + 1))
             stage = ctx.enter_context(tc.tile_pool(name="stage", bufs=2))
             psum = ctx.enter_context(tc.psum_pool(name="psum", bufs=2))
             psum_one = ctx.enter_context(tc.psum_pool(name="psum_one", bufs=1))
-            pools = (keep, win, xin, stage, psum, psum_one)
+            pools = (keep, raw_pool, win, xin, stage, psum, psum_one)
             predictions(nc, pools, x, W_words, W_scales, ident, bias_oc, tile_states)
 
         with ExitStack() as ctx:

@@ -39,14 +39,16 @@ def load_scale_runs(nc, raw_pool, W_scales):
     raw = raw_pool.tile([P, PLANE_WORDS], I32)
     all_words = W_scales.rearrange("g q n -> (g q n)").bitcast(I32)
     for k in range(4):
-        for quadrant in range(4):
-            for j in range(PLANES):
-                partition = 32 * quadrant + 4 * j + k
-                start = j * PLANE_WORDS + 4 * k + 12 * quadrant
-                nc.sync.dma_start(
-                    out=raw[partition : partition + 1, 0:WINDOW_WORDS].rearrange("o (a b) -> o a b", a=16),
-                    in_=all_words[start : start + WINDOW_WORDS].rearrange("(a b) -> a b", a=16).unsqueeze(0),
-                )
+        for odd in range(2):
+            for upper in range(2):
+                for j in range(PLANES):
+                    quadrant = 2 * upper + odd
+                    partition = 32 * quadrant + 4 * j + k
+                    start = j * PLANE_WORDS + 4 * k + 12 * quadrant
+                    nc.sync.dma_start(
+                        out=raw[partition : partition + 1, 0:WINDOW_WORDS].rearrange("o (a b) -> o a b", a=16),
+                        in_=all_words[start : start + WINDOW_WORDS].rearrange("(a b) -> a b", a=16).unsqueeze(0),
+                    )
     return raw
 
 
@@ -137,7 +139,7 @@ def predictions(nc, pools, x, W_words, W_scales, ident, bias_oc, batch_tiles):
                 load_weight_routes(nc, W_words, w_words, first)
                 weights[first] = w_words
             x_sb = xin.tile([P, ROUTES_PER_LOAD, I], BF16)
-            nc.sync.dma_start(out=x_sb[:], in_=x[bt * P : (bt + 1) * P, first : first + ROUTES_PER_LOAD, :])
+            nc.scalar.dma_start(out=x_sb[:], in_=x[bt * P : (bt + 1) * P, first : first + ROUTES_PER_LOAD, :])
             loaded[k + PREFETCH] = x_sb
         if k == 0:
             raw = load_scale_runs(nc, raw_pool, W_scales)
@@ -165,7 +167,8 @@ def predictions(nc, pools, x, W_words, W_scales, ident, bias_oc, batch_tiles):
                 )
 
 
-def squash_factor(nc, small, s, half):
+def squash_norms(nc, small, tile_state, half):
+    s = tile_state["s"]
     squares = small.tile([P, O, C], F32)
     nc.vector.tensor_tensor(out=squares[:], in0=s[:], in1=s[:], op=ALU.mult)
     norm2 = small.tile([P, C], F32)
@@ -175,15 +178,20 @@ def squash_factor(nc, small, s, half):
     inverse = small.tile([P, C], F32)
     nc.vector.tensor_scalar(out=inverse[:], in0=norm2[:], scalar1=1.0, scalar2=EPS, op0=ALU.add, op1=ALU.add)
     nc.vector.reciprocal(out=inverse[:], in_=inverse[:])
+    tile_state["norm"] = norm
+    tile_state["inverse"] = inverse
+
+
+def squash_factor(nc, small, tile_state):
     factor = small.tile([P, C], F32)
-    nc.vector.tensor_tensor(out=factor[:], in0=norm[:], in1=inverse[:], op=ALU.mult)
+    nc.vector.tensor_tensor(out=factor[:], in0=tile_state["norm"][:], in1=tile_state["inverse"][:], op=ALU.mult)
     return factor
 
 
-def squash(nc, pools, tile_state, half):
+def add_squashed(nc, pools, tile_state):
     small, state = pools
     s = tile_state["s"]
-    factor = squash_factor(nc, small, s, half)
+    factor = squash_factor(nc, small, tile_state)
     v = state.tile([P, O, C], F32)
     nc.vector.tensor_tensor(out=v[:], in0=s[:], in1=factor[:].unsqueeze(1).to_broadcast([P, O, C]), op=ALU.mult)
     if "v_sum" in tile_state:
@@ -248,22 +256,28 @@ def route_sums(nc, pools, tile_state, bias_oc):
         out=coupling[:], in0=coupling[:], in1=total[:].unsqueeze(1).to_broadcast([P, C, R]), op=ALU.mult
     )
     s = small.tile([P, O, C], F32)
-    for first in range(0, O, O_PART):
-        weighted = work.tile([P, O_PART, C, R], F32)
-        nc.vector.tensor_tensor(
-            out=weighted[:],
-            in0=u[:, first : first + O_PART, :, :],
-            in1=coupling[:].unsqueeze(1).to_broadcast([P, O_PART, C, R]),
-            op=ALU.mult,
-        )
-        nc.vector.tensor_reduce(out=s[:, first : first + O_PART, :], in_=weighted[:], axis=AX.X, op=ALU.add)
+    parts = {}
+    for first in range(0, O + O_PART, O_PART):
+        if first < O:
+            weighted = work.tile([P, O_PART, C, R], F32)
+            nc.vector.tensor_tensor(
+                out=weighted[:],
+                in0=u[:, first : first + O_PART, :, :],
+                in1=coupling[:].unsqueeze(1).to_broadcast([P, O_PART, C, R]),
+                op=ALU.mult,
+            )
+            parts[first] = weighted
+        if first >= O_PART:
+            nc.vector.tensor_reduce(
+                out=s[:, first - O_PART : first, :], in_=parts[first - O_PART][:], axis=AX.X, op=ALU.add
+            )
     nc.vector.tensor_tensor(out=s[:], in0=s[:], in1=bias_oc[:], op=ALU.add)
     tile_state["s"] = s
 
 
-def store_output(nc, small, tile_state, half, out_rows):
+def store_output(nc, small, tile_state, out_rows):
     s = tile_state["s"]
-    factor = squash_factor(nc, small, s, half)
+    factor = squash_factor(nc, small, tile_state)
     v_out = small.tile([P, C, O], F32)
     nc.vector.tensor_tensor(
         out=v_out[:],
@@ -278,17 +292,23 @@ def routing(nc, pools, ident, half, bias_oc, tile_states, out):
     small, state, work, psum = pools
     turns = [(iteration, bt) for iteration in range(1, ROUTING_ITERS) for bt in range(B_TILES)]
     for bt in range(B_TILES):
-        squash(nc, (small, state), tile_states[bt], half)
+        squash_norms(nc, small, tile_states[bt], half)
+    for bt in range(B_TILES):
+        add_squashed(nc, (small, state), tile_states[bt])
     agreement(nc, (small, work, psum), tile_states[0], ident)
+    exponentials(nc, small, tile_states[0])
     for k, (iteration, bt) in enumerate(turns):
-        exponentials(nc, small, tile_states[bt])
-        if k + 1 < len(turns):
-            agreement(nc, (small, work, psum), tile_states[turns[k + 1][1]], ident)
+        following = tile_states[turns[k + 1][1]] if k + 1 < len(turns) else None
+        if following is not None:
+            agreement(nc, (small, work, psum), following, ident)
         route_sums(nc, (small, work), tile_states[bt], bias_oc)
+        squash_norms(nc, small, tile_states[bt], half)
+        if following is not None:
+            exponentials(nc, small, following)
         if iteration + 1 < ROUTING_ITERS:
-            squash(nc, (small, state), tile_states[bt], half)
+            add_squashed(nc, (small, state), tile_states[bt])
         else:
-            store_output(nc, small, tile_states[bt], half, out[bt * P : (bt + 1) * P])
+            store_output(nc, small, tile_states[bt], out[bt * P : (bt + 1) * P])
 
 
 def tile_capsulelayer_e_kernel(tc, x, W_words, W_scales, bias, out):

@@ -22,7 +22,8 @@ B_TILES = B // P
 ROUTES_PER_LOAD = 8
 ROUTES_PER_BANK = 4
 PAIR = 2
-O_PART = 4
+O_PART = 2
+O_SCALAR = 6
 C_PAIR = 2
 PLANES = 4
 PLANE_ROUTES = R // PLANES
@@ -39,16 +40,14 @@ def load_scale_runs(nc, raw_pool, W_scales):
     raw = raw_pool.tile([P, PLANE_WORDS], I32)
     all_words = W_scales.rearrange("g q n -> (g q n)").bitcast(I32)
     for k in range(4):
-        for odd in range(2):
-            for upper in range(2):
-                for j in range(PLANES):
-                    quadrant = 2 * upper + odd
-                    partition = 32 * quadrant + 4 * j + k
-                    start = j * PLANE_WORDS + 4 * k + 12 * quadrant
-                    nc.sync.dma_start(
-                        out=raw[partition : partition + 1, 0:WINDOW_WORDS].rearrange("o (a b) -> o a b", a=16),
-                        in_=all_words[start : start + WINDOW_WORDS].rearrange("(a b) -> a b", a=16).unsqueeze(0),
-                    )
+        for quadrant in range(4):
+            for j in range(PLANES):
+                partition = 32 * quadrant + 4 * j + k
+                start = j * PLANE_WORDS + 4 * k + 12 * quadrant
+                nc.sync.dma_start(
+                    out=raw[partition : partition + 1, 0:WINDOW_WORDS].rearrange("o (a b) -> o a b", a=16),
+                    in_=all_words[start : start + WINDOW_WORDS].rearrange("(a b) -> a b", a=16).unsqueeze(0),
+                )
     return raw
 
 
@@ -139,7 +138,7 @@ def predictions(nc, pools, x, W_words, W_scales, ident, bias_oc, batch_tiles):
                 load_weight_routes(nc, W_words, w_words, first)
                 weights[first] = w_words
             x_sb = xin.tile([P, ROUTES_PER_LOAD, I], BF16)
-            nc.scalar.dma_start(out=x_sb[:], in_=x[bt * P : (bt + 1) * P, first : first + ROUTES_PER_LOAD, :])
+            nc.sync.dma_start(out=x_sb[:], in_=x[bt * P : (bt + 1) * P, first : first + ROUTES_PER_LOAD, :])
             loaded[k + PREFETCH] = x_sb
         if k == 0:
             raw = load_scale_runs(nc, raw_pool, W_scales)
@@ -267,7 +266,14 @@ def route_sums(nc, pools, tile_state, bias_oc):
                 op=ALU.mult,
             )
             parts[first] = weighted
-        if first >= O_PART:
+        if O_PART <= first <= O_SCALAR:
+            for j in range(O_PART):
+                for c in range(C):
+                    row = parts[first - O_PART][:, j, c, :]
+                    nc.scalar.activation(
+                        out=row, in_=row, func=ACT.Copy, accum_out=s[:, first - O_PART + j, c : c + 1]
+                    )
+        if first > O_SCALAR:
             nc.vector.tensor_reduce(
                 out=s[:, first - O_PART : first, :], in_=parts[first - O_PART][:], axis=AX.X, op=ALU.add
             )
@@ -341,6 +347,6 @@ def tile_capsulelayer_e_kernel(tc, x, W_words, W_scales, bias, out):
         with ExitStack() as ctx:
             small = ctx.enter_context(tc.tile_pool(name="small", bufs=2))
             state = ctx.enter_context(tc.tile_pool(name="state", bufs=(ROUTING_ITERS - 1) * B_TILES))
-            work = ctx.enter_context(tc.tile_pool(name="work", bufs=3))
+            work = ctx.enter_context(tc.tile_pool(name="work", bufs=4))
             psum = ctx.enter_context(tc.psum_pool(name="psum_routing", bufs=2))
             routing(nc, (small, state, work, psum), ident, half, bias_oc, tile_states, out)

from contextlib import ExitStack

import concourse.mybir as mybir
from concourse.masks import make_identity

F32 = mybir.dt.float32
BF16 = mybir.dt.bfloat16
I32 = mybir.dt.int32
U32 = mybir.dt.uint32
U8 = mybir.dt.uint8
FP8X4 = mybir.dt.float8_e4m3fn_x4
ACT = mybir.ActivationFunctionType
ALU = mybir.AluOpType
AX = mybir.AxisListType

P = 128
B, R, C, O, I = 256, 64, 8, 16, 512
CO = C * O
EPS = 1e-8
ROUTING_ITERS = 3
B_TILES = B // P
ROUTES_PER_LOAD = 8
ROUTES_PER_BANK = 4
PAIR = 2
O_PART = 2
O_SCALAR = 6
C_PAIR = 2
PLANES = 4
PLANE_ROUTES = R // PLANES
GROUP_WORDS = 16 * O // 4
PLANE_WORDS = PLANE_ROUTES * C * GROUP_WORDS
WINDOW_WORDS = PLANE_WORDS - 48
PREFETCH = 3
WORD_ROUTES = 4

FLOPS = 2 * B * R * C * O * I


def load_scale_runs(nc, raw_pool, W_scales):
    raw = raw_pool.tile([P, PLANE_WORDS], I32)
    all_words = W_scales.rearrange("g q n -> (g q n)").bitcast(I32)
    for k in range(4):
        for quadrant in range(4):
            for j in range(PLANES):
                partition = 32 * quadrant + 4 * j + k
                start = j * PLANE_WORDS + 4 * k + 12 * quadrant
                nc.sync.dma_start(
                    out=raw[partition : partition + 1, 0:WINDOW_WORDS].rearrange("o (a b) -> o a b", a=16),
                    in_=all_words[start : start + WINDOW_WORDS].rearrange("(a b) -> a b", a=16).unsqueeze(0),
                )
    return raw


def pick_scale_rows(nc, keep, raw):
    w_scales = keep.tile([P, PLANE_ROUTES * CO], U8, align_bytes=64)
    nc.vector.memset(w_scales[:].bitcast(I32), 0)
    for quadrant in range(4):
        rows = slice(32 * quadrant, 32 * quadrant + 4 * PLANES)
        nc.vector.tensor_copy(
            out=w_scales[rows, :].bitcast(I32).rearrange("p (g w) -> p g w", w=O // 4),
            in_=raw[rows, :].rearrange("p (g w) -> p g w", w=GROUP_WORDS)[:, :, 4 * quadrant : 4 * quadrant + O // 4],
        )
    return w_scales


def load_weight_routes(nc, W_words, w_words, first):
    code_words = W_words.rearrange("g p n t -> g p (n t)").bitcast(I32).rearrange("g p w -> p g w")
    for j in range(0, ROUTES_PER_LOAD, WORD_ROUTES):
        nc.sync.dma_start(
            out=w_words[:, j : j + WORD_ROUTES, :].bitcast(I32).rearrange("p r (c w) -> p (r c) w", w=O),
            in_=code_words[:, (first + j) * C : (first + j + WORD_ROUTES) * C, :],
        )


def transpose_routes(nc, pools, copy, x_sb, ident):
    stage, psum = pools
    x_words = x_sb[:].bitcast(F32)
    grouped = stage.tile([P, ROUTES_PER_LOAD, P, 4], BF16, align_bytes=64)
    grouped_words = grouped[:].bitcast(F32)
    for pair in range(ROUTES_PER_LOAD // PAIR):
        xt = psum.tile([P, PAIR, 2, P], F32)
        for j in range(PAIR):
            for h in range(2):
                nc.tensor.transpose(xt[:, j, h, :], x_words[:, pair * PAIR + j, h : I // 2 : 2], ident[:])
        copy(
            out=grouped_words[:, pair * PAIR : (pair + 1) * PAIR, :, :],
            in_=xt[:].rearrange("p j h b -> p j b h"),
        )
    return grouped


def quantise_routes(nc, stage, grouped):
    x_codes = stage.tile([P, ROUTES_PER_LOAD * P], U32, align_bytes=64)
    x_scales = stage.tile([P, ROUTES_PER_LOAD * P], U8, align_bytes=64)
    nc.vector.quantize_mx(
        out=x_codes[:].bitcast(FP8X4),
        scales=x_scales[:],
        in_=grouped[:].rearrange("p r b t -> p (r b t)"),
    )
    return x_codes, x_scales


def multiply_routes(nc, psum, copy, first, x_codes, x_scales, w_words, w_scales, u, route_sum):
    for bank in range(ROUTES_PER_LOAD // ROUTES_PER_BANK):
        u_bank = psum.tile([P, ROUTES_PER_BANK, CO], F32)
        for j in range(ROUTES_PER_BANK):
            slot = bank * ROUTES_PER_BANK + j
            r = first + slot
            operands = dict(
                lhsT=x_codes[:, slot * P : (slot + 1) * P].bitcast(FP8X4),
                lhsT_scale=x_scales[:, slot * P : (slot + 1) * P],
                rhs=w_words[:, slot, :].bitcast(FP8X4),
                rhs_scale=w_scales[4 * (r // PLANE_ROUTES) : P, (r % PLANE_ROUTES) * CO : (r % PLANE_ROUTES + 1) * CO],
            )
            nc.tensor.matmul_mx(out=u_bank[:, j, :], start=True, stop=True, **operands)
            nc.tensor.matmul_mx(out=route_sum[:], start=(r == 0), stop=(r == R - 1), **operands)
        r0 = first + bank * ROUTES_PER_BANK
        copy(
            out=u[:, :, :, r0 : r0 + ROUTES_PER_BANK],
            in_=u_bank[:].rearrange("p r (c o) -> p o c r", o=O),
        )


def predictions(nc, pools, x, W_words, W_scales, ident, bias_oc, batch_tiles):
    keep, raw_pool, win, xin, stage, psum, psum_one = pools
    copies = [nc.scalar.copy, nc.vector.tensor_copy]
    steps = [(bt, first) for first in range(0, R, ROUTES_PER_LOAD) for bt in range(B_TILES)]
    weights = {}
    loaded = {}
    grouped = {}
    quantised = {}
    sum_banks = {}
    for k in range(-PREFETCH, len(steps) + 2):
        if k + PREFETCH < len(steps):
            bt, first = steps[k + PREFETCH]
            if bt == 0:
                w_words = win.tile([P, ROUTES_PER_LOAD, CO], U32, align_bytes=64)
                load_weight_routes(nc, W_words, w_words, first)
                weights[first] = w_words
            x_sb = xin.tile([P, ROUTES_PER_LOAD, I], BF16)
            nc.sync.dma_start(out=x_sb[:], in_=x[bt * P : (bt + 1) * P, first : first + ROUTES_PER_LOAD, :])
            loaded[k + PREFETCH] = x_sb
        if k == 0:
            raw = load_scale_runs(nc, raw_pool, W_scales)
        if 0 <= k < len(steps):
            grouped[k] = transpose_routes(nc, (stage, psum), copies[steps[k][0]], loaded[k], ident)
        if 1 <= k <= len(steps):
            quantised[k - 1] = quantise_routes(nc, stage, grouped[k - 1])
        if k == 2:
            w_scales = pick_scale_rows(nc, keep, raw)
        if k >= 2:
            bt, first = steps[k - 2]
            u, s = batch_tiles[bt]["u"], batch_tiles[bt]["s"]
            if first == 0:
                sum_banks[bt] = psum_one.tile([P, CO], F32, name="route_sum%d" % bt)
            x_codes, x_scales = quantised[k - 2]
            multiply_routes(nc, psum, copies[bt], first, x_codes, x_scales, weights[first], w_scales, u, sum_banks[bt])
            if first + ROUTES_PER_LOAD == R:
                nc.vector.scalar_tensor_tensor(
                    out=s[:],
                    in0=sum_banks[bt][:].rearrange("p (c o) -> p o c", o=O),
                    scalar=1.0 / C,
                    in1=bias_oc[:],
                    op0=ALU.mult,
                    op1=ALU.add,
                )


def squash_norms(nc, small, tile_state, half):
    s = tile_state["s"]
    squares = small.tile([P, O, C], F32)
    nc.vector.tensor_tensor(out=squares[:], in0=s[:], in1=s[:], op=ALU.mult)
    norm2 = small.tile([P, C], F32)
    nc.vector.tensor_reduce(out=norm2[:], in_=squares[:].rearrange("p o c -> p c o"), axis=AX.X, op=ALU.add)
    norm = small.tile([P, C], F32)
    nc.gpsimd.tensor_tensor(out=norm[:], in0=norm2[:], in1=half[:], op=ALU.pow)
    inverse = small.tile([P, C], F32)
    nc.vector.tensor_scalar(out=inverse[:], in0=norm2[:], scalar1=1.0, scalar2=EPS, op0=ALU.add, op1=ALU.add)
    nc.vector.reciprocal(out=inverse[:], in_=inverse[:])
    tile_state["norm"] = norm
    tile_state["inverse"] = inverse


def squash_factor(nc, small, tile_state):
    factor = small.tile([P, C], F32)
    nc.vector.tensor_tensor(out=factor[:], in0=tile_state["norm"][:], in1=tile_state["inverse"][:], op=ALU.mult)
    return factor


def add_squashed(nc, pools, tile_state):
    small, state = pools
    s = tile_state["s"]
    factor = squash_factor(nc, small, tile_state)
    v = state.tile([P, O, C], F32)
    nc.vector.tensor_tensor(out=v[:], in0=s[:], in1=factor[:].unsqueeze(1).to_broadcast([P, O, C]), op=ALU.mult)
    if "v_sum" in tile_state:
        nc.vector.tensor_tensor(out=v[:], in0=v[:], in1=tile_state["v_sum"][:], op=ALU.add)
    tile_state["v_sum"] = v


def agreement(nc, pools, tile_state, ident):
    small, work, psum = pools
    u = tile_state["u"]
    v_sum = tile_state["v_sum"]
    logits_t = psum.tile([P, C // C_PAIR, P], F32)
    for pair in range(C // C_PAIR):
        products = work.tile([P, O, C_PAIR, R], F32)
        for o in range(O):
            for j in range(C_PAIR):
                c = pair * C_PAIR + j
                nc.scalar.activation(
                    out=products[:, o, j, :], in_=u[:, o, c, :], func=ACT.Copy, scale=v_sum[:, o, c : c + 1]
                )
        for o in range(O):
            nc.tensor.matmul(
                out=logits_t[:, pair, :],
                lhsT=products[:, o, :, :].rearrange("p j r -> p (j r)"),
                rhs=ident[:],
                is_transpose=True,
                start=(o == 0),
                stop=(o == O - 1),
            )
    logits_t_sb = small.tile([P, C // C_PAIR, P], F32)
    nc.scalar.copy(out=logits_t_sb[:], in_=logits_t[:])
    logits = psum.tile([P, C, R], F32)
    for pair in range(C // C_PAIR):
        nc.tensor.transpose(
            logits[:, pair * C_PAIR : (pair + 1) * C_PAIR, :].rearrange("p j r -> p (j r)"),
            logits_t_sb[:, pair, :],
            ident[:],
        )
    tile_state["logits"] = logits


def exponentials(nc, small, tile_state):
    logits = tile_state["logits"]
    top = small.tile([P, R], F32)
    nc.vector.tensor_reduce(out=top[:], in_=logits[:].rearrange("p c r -> p r c"), axis=AX.X, op=ALU.max)
    coupling = small.tile([P, C, R], F32)
    nc.vector.tensor_tensor(
        out=coupling[:], in0=logits[:], in1=top[:].unsqueeze(1).to_broadcast([P, C, R]), op=ALU.subtract
    )
    nc.scalar.activation(out=coupling[:], in_=coupling[:], func=ACT.Exp)
    tile_state["coupling"] = coupling


def route_sums(nc, pools, tile_state, bias_oc):
    small, work = pools
    u = tile_state["u"]
    coupling = tile_state["coupling"]
    total = small.tile([P, R], F32)
    nc.vector.tensor_reduce(out=total[:], in_=coupling[:].rearrange("p c r -> p r c"), axis=AX.X, op=ALU.add)
    nc.vector.reciprocal(out=total[:], in_=total[:])
    nc.vector.tensor_tensor(
        out=coupling[:], in0=coupling[:], in1=total[:].unsqueeze(1).to_broadcast([P, C, R]), op=ALU.mult
    )
    s = small.tile([P, O, C], F32)
    parts = {}
    for first in range(0, O + O_PART, O_PART):
        if first < O:
            weighted = work.tile([P, O_PART, C, R], F32)
            nc.vector.tensor_tensor(
                out=weighted[:],
                in0=u[:, first : first + O_PART, :, :],
                in1=coupling[:].unsqueeze(1).to_broadcast([P, O_PART, C, R]),
                op=ALU.mult,
            )
            parts[first] = weighted
        if O_PART <= first <= O_SCALAR:
            for j in range(O_PART):
                for c in range(C):
                    row = parts[first - O_PART][:, j, c, :]
                    nc.scalar.activation(
                        out=row, in_=row, func=ACT.Copy, accum_out=s[:, first - O_PART + j, c : c + 1]
                    )
        if first > O_SCALAR:
            nc.vector.tensor_reduce(
                out=s[:, first - O_PART : first, :], in_=parts[first - O_PART][:], axis=AX.X, op=ALU.add
            )
    nc.vector.tensor_tensor(out=s[:], in0=s[:], in1=bias_oc[:], op=ALU.add)
    tile_state["s"] = s


def store_output(nc, small, tile_state, out_rows):
    s = tile_state["s"]
    factor = squash_factor(nc, small, tile_state)
    v_out = small.tile([P, C, O], F32)
    nc.vector.tensor_tensor(
        out=v_out[:],
        in0=s[:].rearrange("p o c -> p c o"),
        in1=factor[:].unsqueeze(2).to_broadcast([P, C, O]),
        op=ALU.mult,
    )
    nc.sync.dma_start(out=out_rows.rearrange("b c o -> b (c o)"), in_=v_out[:].rearrange("p c o -> p (c o)"))


def routing(nc, pools, ident, half, bias_oc, tile_states, out):
    small, state, work, psum = pools
    turns = [(iteration, bt) for iteration in range(1, ROUTING_ITERS) for bt in range(B_TILES)]
    for bt in range(B_TILES):
        squash_norms(nc, small, tile_states[bt], half)
    for bt in range(B_TILES):
        add_squashed(nc, (small, state), tile_states[bt])
    agreement(nc, (small, work, psum), tile_states[0], ident)
    exponentials(nc, small, tile_states[0])
    for k, (iteration, bt) in enumerate(turns):
        following = tile_states[turns[k + 1][1]] if k + 1 < len(turns) else None
        if following is not None:
            agreement(nc, (small, work, psum), following, ident)
        route_sums(nc, (small, work), tile_states[bt], bias_oc)
        squash_norms(nc, small, tile_states[bt], half)
        if following is not None:
            exponentials(nc, small, following)
        if iteration + 1 < ROUTING_ITERS:
            add_squashed(nc, (small, state), tile_states[bt])
        else:
            store_output(nc, small, tile_states[bt], out[bt * P : (bt + 1) * P])


def tile_capsulelayer_e_kernel(tc, x, W_words, W_scales, bias, out):
    nc = tc.nc
    with tc.tile_pool(name="keep", bufs=1) as keep:
        ident = keep.tile([P, P], F32)
        make_identity(nc, ident[:])
        half = keep.tile([P, C], F32)
        nc.gpsimd.memset(half[:], 0.5)
        bias_rows = keep.tile([P, CO], BF16)
        nc.sync.dma_start(out=bias_rows[:], in_=bias.rearrange("a b c o -> (a b c o)").partition_broadcast(P))
        bias_oc = keep.tile([P, O, C], F32)
        nc.vector.tensor_copy(out=bias_oc[:], in_=bias_rows[:].rearrange("p (c o) -> p o c", o=O))
        tile_states = []
        for bt in range(B_TILES):
            u = keep.tile([P, O, C, R], F32, name="u%d" % bt)
            s = keep.tile([P, O, C], F32, name="s%d" % bt)
            tile_states.append({"u": u, "s": s})

        with ExitStack() as ctx:
            raw_pool = ctx.enter_context(tc.tile_pool(name="raw", bufs=1))
            win = ctx.enter_context(tc.tile_pool(name="win", bufs=4))
            xin = ctx.enter_context(tc.tile_pool(name="xin", bufs=PREFETCH + 1))
            stage = ctx.enter_context(tc.tile_pool(name="stage", bufs=2))
            psum = ctx.enter_context(tc.psum_pool(name="psum", bufs=2))
            psum_one = ctx.enter_context(tc.psum_pool(name="psum_one", bufs=1))
            pools = (keep, raw_pool, win, xin, stage, psum, psum_one)
            predictions(nc, pools, x, W_words, W_scales, ident, bias_oc, tile_states)

        with ExitStack() as ctx:
            small = ctx.enter_context(tc.tile_pool(name="small", bufs=2))
            state = ctx.enter_context(tc.tile_pool(name="state", bufs=(ROUTING_ITERS - 1) * B_TILES))
            work = ctx.enter_context(tc.tile_pool(name="work", bufs=4))
            psum = ctx.enter_context(tc.psum_pool(name="psum_routing", bufs=2))
            routing(nc, (small, state, work, psum), ident, half, bias_oc, tile_states, out)
